import numpy as np
import ml_dtypes


def mxq(x, axis, fmt="e4m3"):
    dtype, down = {"e4m3": (ml_dtypes.float8_e4m3fn, 7), "e5m2": (ml_dtypes.float8_e5m2, 14)}[fmt]
    v = np.moveaxis(np.asarray(x, np.float32).astype(ml_dtypes.bfloat16).astype(np.float64), axis, -1)
    blocks = v.reshape(v.shape[:-1] + (-1, 32))
    amax = np.abs(blocks).max(-1, keepdims=True)
    byte = np.maximum(np.where(amax > 0, np.frexp(amax)[1] - 1 + 127, 0) - down, 1)
    scale = np.exp2(byte - 127.0)
    codes = (blocks / scale).astype(np.float32).astype(dtype).astype(np.float64)
    return np.moveaxis((codes * scale).reshape(v.shape), -1, axis)


WIDE = False


def mx_kscale(k):
    if not WIDE:
        return np.ones(k)
    levels = np.array([10, -10, 5, -5, 0])
    if k % 512:
        return np.exp2(np.random.permutation(np.resize(levels, k // 32))).repeat(32)
    a = np.empty((k // 512, 16))
    for p in range(k // 512):
        a[p, :8] = np.random.permutation(np.resize(levels, 8))
        for g in range(8):
            far = levels[np.abs(levels - a[p, g]) >= 10]
            a[p, g + 8] = far[np.random.randint(len(far))]
    return np.exp2(a.ravel()).repeat(32)


BF16 = ml_dtypes.bfloat16


def bf(x):
    return np.asarray(x, np.float32).astype(BF16)


def f64(x):
    return np.asarray(x).astype(np.float64)


W, M, K, N = 4, 512, 2048, 1024


def setup_inputs():
    s = mx_kscale(K)
    return {"x": bf(np.random.standard_normal((W, M, K)) * s),
            "weight": bf(np.random.standard_normal((W, N, K)) / np.sqrt(W * K) / s),
            "bias": bf(np.random.standard_normal((W, M, N)) / np.sqrt(W))}


def core(x, weight, bias):
    w, m, _ = x.shape
    xq = mxq(f64(x), 2, "e4m3")
    wq = mxq(f64(weight), 2, "e4m3")
    y = (xq @ wq.transpose(0, 2, 1)).sum(0) + f64(bias).sum(0)
    m_per_rank = m // w
    return y.reshape(w, m_per_rank, -1)


def e4m3fn_bytes(y):
    return np.clip(np.asarray(y, np.float64), -448.0, 448.0).astype(np.float32).astype(ml_dtypes.float8_e4m3fn).view(np.uint8)


def reference(x, weight, bias):
    out = core(x, weight, bias)
    s = np.max(np.abs(out), axis=-1, keepdims=True) / 448.0
    return out, e4m3fn_bytes(out / s)

@@ -1,0 +1,353 @@
+from contextlib import ExitStack
+
+import concourse.mybir as mybir
+from concourse.masks import make_identity
+
+FLOPS = 2 * 512 * 1024 * 8192
+
+F32 = mybir.dt.float32
+BF16 = mybir.dt.bfloat16
+U32 = mybir.dt.uint32
+U8 = mybir.dt.uint8
+FP8 = mybir.dt.float8_e4m3fn
+FP8X4 = mybir.dt.float8_e4m3fn_x4
+ALU = mybir.AluOpType
+ACT = mybir.ActivationFunctionType
+AX = mybir.AxisListType
+
+P = 128
+NRUN = 24
+NB_RAW = 6
+PA = 2
+LAG = 2
+NS = 3
+FIRST2 = 16 + LAG
+TAIL_STEP = 23
+
+
+def pre_pattern(i):
+    if i < 3:
+        return "----"
+    if i < 20:
+        return "VVV-"
+    return "VVSS"
+
+
+def tile_gemmrstritonpcie_kernel(tc, x, weight, bias, out_0, out_1):
+    nc = tc.nc
+    with ExitStack() as ctx:
+        const = ctx.enter_context(tc.tile_pool(name="const", bufs=1))
+        keep = ctx.enter_context(tc.tile_pool(name="keep", bufs=1))
+        rawp = ctx.enter_context(tc.tile_pool(name="rawp", bufs=NB_RAW))
+        prep = ctx.enter_context(tc.tile_pool(name="prep", bufs=6))
+        grp = ctx.enter_context(tc.tile_pool(name="grp", bufs=6))
+        wcp = ctx.enter_context(tc.tile_pool(name="wcp", bufs=8))
+        bp = ctx.enter_context(tc.tile_pool(name="bp", bufs=4))
+        tmp = ctx.enter_context(tc.tile_pool(name="tmp", bufs=2))
+        o1p = ctx.enter_context(tc.tile_pool(name="o1p", bufs=4))
+        trp = ctx.enter_context(tc.psum_pool(name="trp", bufs=4))
+        accp = ctx.enter_context(tc.psum_pool(name="accp", bufs=1))
+
+        ident = const.tile([P, P], F32, name="ident", tag="ident")
+        make_identity(nc, ident[:])
+        zeros = const.tile([P, 1], F32, name="zeros", tag="zeros")
+        nc.vector.memset(zeros[:], 0.0)
+        warm = const.tile([P, 1], F32, name="warm", tag="warm")
+        st = const.tile([P, 8], F32, name="st", tag="st")
+        sc = const.tile([P, 4], F32, name="sc", tag="sc")
+        fac = const.tile([P, 4], F32, name="fac", tag="fac")
+
+        xc = keep.tile([P, 16, 512], U32, name="xc", tag="xc", align_bytes=64)
+        xs = keep.tile([P, 16, 512], U8, name="xs", tag="xs", align_bytes=64)
+        bs = []
+        o0 = []
+        for mt in range(4):
+            bs_t = keep.tile([P, 1024], F32, name="bs%d" % mt, tag="bs%d" % mt)
+            o0_t = keep.tile([P, 1024], F32, name="o0%d" % mt, tag="o0%d" % mt)
+            bs.append(bs_t)
+            o0.append(o0_t)
+
+        ctx.enter_context(tc.manual_schedule())
+
+        nc.scalar.activation(out=warm[:], in_=zeros[:], func=ACT.Identity,
+                             bias=zeros[:, 0:1], scale=zeros[:, 0:1])
+
+        runs = []
+        for g in range(16):
+            runs.append([("x", 0, g, ("x", 0, g // 2), g % 2), ("w", 0, g, ("w", 0, g // 2), g % 2)])
+        for s in range(8):
+            runs.append([("w", 1, 2 * s + a, ("w", 1, s), a) for a in range(2)])
+        load_seq = []
+        for s in range(8):
+            load_seq.append(("x", 0, s))
+            load_seq.append(("w", 0, s))
+        for s in range(8):
+            load_seq.append(("w", 1, s))
+
+        def last_use(j):
+            return 2 * (j // 2) + 1 if j < 16 else j
+
+        raws = {}
+        pres = {}
+        wcodes = {}
+        braws = {}
+        accs = {}
+        tsum = {}
+        state = {"next_load": 0}
+
+        def dram_rows(key, ks):
+            op, half, stage = key
+            rank = stage // 2
+            if op == "x":
+                src = x[rank, :, ks]
+            else:
+                src = weight[rank, 512 * half:512 * (half + 1), ks]
+            return src.rearrange("(t p) k -> p t k", p=P)
+
+        def load_whole(key):
+            k0 = 1024 * (key[2] % 2)
+            raw = rawp.tile([P, 4, 1024], BF16, name="raw", tag="raw")
+            nc.sync.dma_start(out=raw[:], in_=dram_rows(key, slice(k0, k0 + 1024)))
+            raws[key] = (raw, False)
+
+        def load_split_pair(stage):
+            tiles = []
+            for op in ("x", "w"):
+                raw = rawp.tile([P, 2, 4, 512], BF16, name="raw", tag="raw")
+                raws[(op, 0, stage)] = (raw, True)
+                tiles.append(((op, 0, stage), raw))
+            k0 = 1024 * (stage % 2)
+            for a in range(2):
+                for key, raw in tiles:
+                    nc.sync.dma_start(out=raw[:, a, :, :],
+                                      in_=dram_rows(key, slice(k0 + 512 * a, k0 + 512 * (a + 1))))
+
+        def free_slot(j, i):
+            return j < NB_RAW or last_use(j - NB_RAW) <= i - 1
+
+        def emit_loads(i):
+            while state["next_load"] < NRUN and free_slot(state["next_load"], i):
+                j = state["next_load"]
+                if j < 2 * NS and j % 2 == 0:
+                    if not free_slot(j + 1, i):
+                        break
+                    load_split_pair(j // 2)
+                    state["next_load"] = j + 2
+                else:
+                    load_whole(load_seq[j])
+                    state["next_load"] = j + 1
+
+        def unit_words(unit, t0, nt):
+            raw, split = raws[unit[3]]
+            a = unit[4]
+            if split:
+                return raw[:, a, t0:t0 + nt, :].bitcast(F32)
+            return raw[:, t0:t0 + nt, 512 * a:512 * (a + 1)].bitcast(F32)
+
+        def pre_tile(unit):
+            uid = unit[0:3]
+            if uid not in pres:
+                pt = prep.tile([P, 4, 2, P], F32, name="pt", tag="pt")
+                pres[uid] = pt
+            return pres[uid]
+
+        def pre_piece(unit, t0, nt, eng):
+            pt = pre_tile(unit)
+            src = unit_words(unit, t0, nt).rearrange("p t (w u) -> p t u w", u=2)
+            if eng == "V":
+                nc.vector.tensor_copy(out=pt[:, t0:t0 + nt, :, :], in_=src)
+            else:
+                nc.scalar.copy(out=pt[:, t0:t0 + nt, :, :], in_=src)
+
+        def pre_vector(j, which):
+            if j >= NRUN:
+                return
+            pat = pre_pattern(j)
+            tps = [tp for tp in range(2) if pat[2 * which + tp] == "V"]
+            if tps:
+                pre_piece(runs[j][which], 2 * tps[0], 2 * len(tps), "V")
+
+        def pre_scalar_list(j):
+            if j >= NRUN:
+                return []
+            pat = pre_pattern(j)
+            return [(runs[j][k // 2], k % 2) for k in range(4) if pat[k] == "S"]
+
+        def bank(i, k, g):
+            unit = runs[i][k // 2]
+            tp = k % 2
+            tr = trp.tile([P, 2, 2, P], F32, name="tr", tag="tr")
+            for tt in range(2):
+                for u in range(2):
+                    if pre_pattern(i)[k] == "-":
+                        src = unit_words(unit, 2 * tp + tt, 1)[:, 0, u:256:2]
+                    else:
+                        src = pres[unit[0:3]][:, 2 * tp + tt, u, :]
+                    nc.tensor.transpose(tr[:, tt, u, :], src, ident[:])
+            gw = g[:].bitcast(F32)
+            nc.scalar.copy(
+                out=gw[:, 512 * tp:512 * (tp + 1)].rearrange("p (tt r u) -> p tt r u", tt=2, u=2),
+                in_=tr[:].rearrange("p tt u r -> p tt r u"),
+            )
+
+        def quantize(unit, g):
+            op, half, g_pass = unit[0:3]
+            if op == "x":
+                codes = xc[:, g_pass, :]
+                scl = xs[:, g_pass, :]
+            else:
+                wc = wcp.tile([P, 512], U32, name="wc", tag="wc", align_bytes=64)
+                ws = wcp.tile([P, 512], U8, name="ws", tag="ws", align_bytes=64)
+                wcodes[(half, g_pass)] = (wc, ws)
+                codes = wc[:]
+                scl = ws[:]
+            nc.vector.quantize_mx(out=codes.bitcast(FP8X4), scales=scl, in_=g[:])
+
+        def mm(half, g_pass, mt):
+            wc, ws = wcodes[(half, g_pass)]
+            nc.tensor.matmul_mx(
+                out=accs[(half, mt)][:],
+                lhsT=xc[:, g_pass, P * mt:P * (mt + 1)].bitcast(FP8X4),
+                lhsT_scale=xs[:, g_pass, P * mt:P * (mt + 1)],
+                rhs=wc[:].bitcast(FP8X4),
+                rhs_scale=ws[:],
+                start=(g_pass == 0),
+                stop=(g_pass == 15),
+            )
+
+        def alloc_acc(half):
+            for mt in range(4):
+                acc = accp.tile([P, 512], F32, name="acc%d" % mt, tag="acc%d" % mt)
+                accs[(half, mt)] = acc
+
+        def bias_load(mt, half):
+            braw = bp.tile([P, 4, 512], BF16, name="braw", tag="braw")
+            nc.sync.dma_start(out=braw[:], in_=bias[:, P * mt:P * (mt + 1), 512 * half:512 * (half + 1)]
+                              .rearrange("r p n -> p r n"))
+            braws[(mt, half)] = braw
+
+        def bias_sum(mt, half, part):
+            braw = braws[(mt, half)]
+            if part == 0:
+                t01 = tmp.tile([P, 512], F32, name="t01", tag="t01")
+                nc.vector.tensor_tensor(out=t01[:], in0=braw[:, 0, :], in1=braw[:, 1, :], op=ALU.add)
+                tsum[(mt, half, 0)] = t01
+            elif part == 1:
+                t23 = tmp.tile([P, 512], F32, name="t23", tag="t23")
+                nc.vector.tensor_tensor(out=t23[:], in0=braw[:, 2, :], in1=braw[:, 3, :], op=ALU.add)
+                tsum[(mt, half, 1)] = t23
+            else:
+                nc.vector.tensor_tensor(out=bs[mt][:, 512 * half:512 * (half + 1)],
+                                        in0=tsum[(mt, half, 0)][:], in1=tsum[(mt, half, 1)][:], op=ALU.add)
+
+        def ev_add(half, mt):
+            cs = slice(512 * half, 512 * (half + 1))
+            nc.vector.tensor_tensor(out=o0[mt][:, cs], in0=accs[(half, mt)][:], in1=bs[mt][:, cs], op=ALU.add)
+
+        def store0(half, mt):
+            cs = slice(512 * half, 512 * (half + 1))
+            nc.sync.dma_start(out=out_0[mt, :, cs], in_=o0[mt][:, cs])
+
+        def ev_red(half, mt):
+            cs = slice(512 * half, 512 * (half + 1))
+            nc.vector.tensor_reduce(out=st[:, 2 * mt + half:2 * mt + half + 1], in_=o0[mt][:, cs],
+                                    axis=AX.X, op=ALU.max, apply_absolute_value=True)
+
+        def factor(mt):
+            nc.vector.tensor_scalar(out=sc[:, mt:mt + 1], in0=st[:, 2 * mt:2 * mt + 1],
+                                    scalar1=st[:, 2 * mt + 1:2 * mt + 2], scalar2=1.0 / 448.0,
+                                    op0=ALU.max, op1=ALU.mult)
+            nc.vector.reciprocal(out=fac[:, mt:mt + 1], in_=sc[:, mt:mt + 1])
+
+        def cast_store(mt, vcols):
+            o1 = o1p.tile([P, 1024], FP8, name="o1", tag="o1")
+            if vcols > 0:
+                nc.vector.tensor_scalar(out=o1[:, 0:vcols], in0=o0[mt][:, 0:vcols],
+                                        scalar1=fac[:, mt:mt + 1], scalar2=None, op0=ALU.mult,
+                                        saturate=False)
+            nc.scalar.activation(out=o1[:, vcols:1024], in_=o0[mt][:, vcols:1024], func=ACT.Identity,
+                                 bias=zeros[:, 0:1], scale=fac[:, mt:mt + 1], saturate=False)
+            nc.sync.dma_start(out=out_1[mt], in_=o1[:].bitcast(U8))
+
+        v_extra = {}
+        todo = [(mt, 0, part) for mt in range(4) for part in range(3)]
+        for n, item in enumerate(todo):
+            v_extra.setdefault(4 + n, []).append(item)
+        todo = [(mt, 1, part) for mt in range(4) for part in range(3)]
+        for n, item in enumerate(todo):
+            v_extra.setdefault(17 + n // 2, []).append(item)
+        b_load = {}
+        for step in sorted(v_extra):
+            for mt, half, part in v_extra[step]:
+                if part == 0:
+                    b_load.setdefault(step - 2, []).append((mt, half))
+
+        emit_loads(0)
+        alloc_acc(0)
+        for j in range(PA):
+            pre_vector(j, 0)
+            pre_vector(j, 1)
+        for i in range(NRUN):
+            emit_loads(i)
+            for mt, half in b_load.get(i, []):
+                bias_load(mt, half)
+            j = i + PA
+            s_list = pre_scalar_list(j)
+            pre_vector(j, 0)
+            g0 = grp.tile([P, 2048], BF16, name="g", tag="g", align_bytes=64)
+            g1 = grp.tile([P, 2048], BF16, name="g", tag="g", align_bytes=64)
+            gs = [g0, g1]
+            for k in range(4):
+                bank(i, k, gs[k // 2])
+                if s_list:
+                    unit, tp = s_list[0]
+                    s_list = s_list[1:]
+                    pre_piece(unit, 2 * tp, 2, "S")
+            if LAG <= i < FIRST2:
+                for mt in range(4):
+                    mm(0, i - LAG, mt)
+            elif FIRST2 <= i < TAIL_STEP:
+                if i == FIRST2:
+                    alloc_acc(1)
+                for g_pass in (2 * (i - FIRST2), 2 * (i - FIRST2) + 1):
+                    for mt in range(4):
+                        mm(1, g_pass, mt)
+            quantize(runs[i][0], g0)
+            pre_vector(j, 1)
+            if i == FIRST2 - 1:
+                for mt in range(4):
+                    ev_add(0, mt)
+            quantize(runs[i][1], g1)
+            if i == FIRST2 - 1:
+                for mt in range(4):
+                    store0(0, mt)
+            if FIRST2 <= i < FIRST2 + 4:
+                ev_red(0, i - FIRST2)
+            for mt, half, part in v_extra.get(i, []):
+                bias_sum(mt, half, part)
+
+        d = 2 * (TAIL_STEP - FIRST2)
+        for mt in (0, 1):
+            for g_pass in range(d, 14):
+                mm(1, g_pass, mt)
+        for mt in (0, 1):
+            for g_pass in range(14, 16):
+                mm(1, g_pass, mt)
+        ev_add(1, 0)
+        store0(1, 0)
+        ev_add(1, 1)
+        store0(1, 1)
+        ev_red(1, 0)
+        ev_red(1, 1)
+        factor(0)
+        cast_store(0, 0)
+        factor(1)
+        cast_store(1, 0)
+        for mt in (2, 3):
+            for g_pass in range(d, 16):
+                mm(1, g_pass, mt)
+            ev_add(1, mt)
+            store0(1, mt)
+            ev_red(1, mt)
+            factor(mt)
+            cast_store(mt, 0 if mt == 2 else 640)

@@ -20,7 +20,7 @@ NRUN = 24
 NB_RAW = 6
 PA = 2
 LAG = 2
-NS = 3
+NS = 1
 FIRST2 = 16 + LAG
 TAIL_STEP = 23
 

@@ -20,13 +20,13 @@ NRUN = 24
 NB_RAW = 6
 PA = 2
 LAG = 2
-NS = 1
+NE = 2
 FIRST2 = 16 + LAG
 TAIL_STEP = 23
 
 
 def pre_pattern(i):
-    if i < 3:
+    if i < 4:
         return "----"
     if i < 20:
         return "VVV-"
@@ -73,7 +73,10 @@ def tile_gemmrstritonpcie_kernel(tc, x, weight, bias, out_0, out_1):
                              bias=zeros[:, 0:1], scale=zeros[:, 0:1])
 
         runs = []
-        for g in range(16):
+        for s in range(NE):
+            for op in ("x", "w"):
+                runs.append([(op, 0, 2 * s + a, (op, 0, s), a) for a in range(2)])
+        for g in range(2 * NE, 16):
             runs.append([("x", 0, g, ("x", 0, g // 2), g % 2), ("w", 0, g, ("w", 0, g // 2), g % 2)])
         for s in range(8):
             runs.append([("w", 1, 2 * s + a, ("w", 1, s), a) for a in range(2)])
@@ -85,6 +88,8 @@ def tile_gemmrstritonpcie_kernel(tc, x, weight, bias, out_0, out_1):
             load_seq.append(("w", 1, s))
 
         def last_use(j):
+            if j < 2 * NE:
+                return j
             return 2 * (j // 2) + 1 if j < 16 else j
 
         raws = {}
@@ -110,17 +115,13 @@ def tile_gemmrstritonpcie_kernel(tc, x, weight, bias, out_0, out_1):
             nc.sync.dma_start(out=raw[:], in_=dram_rows(key, slice(k0, k0 + 1024)))
             raws[key] = (raw, False)
 
-        def load_split_pair(stage):
-            tiles = []
-            for op in ("x", "w"):
-                raw = rawp.tile([P, 2, 4, 512], BF16, name="raw", tag="raw")
-                raws[(op, 0, stage)] = (raw, True)
-                tiles.append(((op, 0, stage), raw))
-            k0 = 1024 * (stage % 2)
-            for a in range(2):
-                for key, raw in tiles:
-                    nc.sync.dma_start(out=raw[:, a, :, :],
-                                      in_=dram_rows(key, slice(k0 + 512 * a, k0 + 512 * (a + 1))))
+        def load_pieces(key, cuts):
+            k0 = 1024 * (key[2] % 2)
+            raw = rawp.tile([P, 4, 1024], BF16, name="raw", tag="raw")
+            src = dram_rows(key, slice(k0, k0 + 1024))
+            for t0, t1 in cuts:
+                nc.sync.dma_start(out=raw[:, t0:t1, :], in_=src[:, t0:t1, :])
+            raws[key] = (raw, False)
 
         def free_slot(j, i):
             return j < NB_RAW or last_use(j - NB_RAW) <= i - 1
@@ -128,14 +129,13 @@ def tile_gemmrstritonpcie_kernel(tc, x, weight, bias, out_0, out_1):
         def emit_loads(i):
             while state["next_load"] < NRUN and free_slot(state["next_load"], i):
                 j = state["next_load"]
-                if j < 2 * NS and j % 2 == 0:
-                    if not free_slot(j + 1, i):
-                        break
-                    load_split_pair(j // 2)
-                    state["next_load"] = j + 2
+                if j == 0:
+                    load_pieces(load_seq[j], [(0, 1), (1, 2), (2, 4)])
+                elif j < 2 * NE:
+                    load_pieces(load_seq[j], [(0, 2), (2, 4)])
                 else:
                     load_whole(load_seq[j])
-                    state["next_load"] = j + 1
+                state["next_load"] = j + 1
 
         def unit_words(unit, t0, nt):
             raw, split = raws[unit[3]]
@@ -297,7 +297,7 @@ def tile_gemmrstritonpcie_kernel(tc, x, weight, bias, out_0, out_1):
             g0 = grp.tile([P, 2048], BF16, name="g", tag="g", align_bytes=64)
             g1 = grp.tile([P, 2048], BF16, name="g", tag="g", align_bytes=64)
             gs = [g0, g1]
-            for k in range(4):
+            for k in ((0, 2, 1, 3) if i < 2 * NE else (0, 1, 2, 3)):
                 bank(i, k, gs[k // 2])
                 if s_list:
                     unit, tp = s_list[0]

@@ -16,21 +16,22 @@ ACT = mybir.ActivationFunctionType
 AX = mybir.AxisListType
 
 P = 128
-NRUN = 24
+NT = 24
 NB_RAW = 6
-PA = 2
-LAG = 2
-NE = 2
-FIRST2 = 16 + LAG
-TAIL_STEP = 23
+NB_PRE = 3
+NPLAIN = 5
+PA = 1
+B0_START = 5
+B1_START = 18
+B_LEAD = 3
 
 
-def pre_pattern(i):
-    if i < 4:
-        return "----"
-    if i < 20:
-        return "VVV-"
-    return "VVSS"
+def shares(i):
+    if i < NPLAIN:
+        return (0, 0)
+    if i < 16:
+        return (3, 0)
+    return (2, 2)
 
 
 def tile_gemmrstritonpcie_kernel(tc, x, weight, bias, out_0, out_1):
@@ -39,9 +40,10 @@ def tile_gemmrstritonpcie_kernel(tc, x, weight, bias, out_0, out_1):
         const = ctx.enter_context(tc.tile_pool(name="const", bufs=1))
         keep = ctx.enter_context(tc.tile_pool(name="keep", bufs=1))
         rawp = ctx.enter_context(tc.tile_pool(name="rawp", bufs=NB_RAW))
-        prep = ctx.enter_context(tc.tile_pool(name="prep", bufs=6))
-        grp = ctx.enter_context(tc.tile_pool(name="grp", bufs=6))
-        wcp = ctx.enter_context(tc.tile_pool(name="wcp", bufs=8))
+        prep = ctx.enter_context(tc.tile_pool(name="prep", bufs=NB_PRE))
+        gwp = ctx.enter_context(tc.tile_pool(name="gwp", bufs=2))
+        gxp = ctx.enter_context(tc.tile_pool(name="gxp", bufs=2))
+        wcp = ctx.enter_context(tc.tile_pool(name="wcp", bufs=3))
         bp = ctx.enter_context(tc.tile_pool(name="bp", bufs=4))
         tmp = ctx.enter_context(tc.tile_pool(name="tmp", bufs=2))
         o1p = ctx.enter_context(tc.tile_pool(name="o1p", bufs=4))
@@ -57,14 +59,11 @@ def tile_gemmrstritonpcie_kernel(tc, x, weight, bias, out_0, out_1):
         sc = const.tile([P, 4], F32, name="sc", tag="sc")
         fac = const.tile([P, 4], F32, name="fac", tag="fac")
 
-        xc = keep.tile([P, 16, 512], U32, name="xc", tag="xc", align_bytes=64)
-        xs = keep.tile([P, 16, 512], U8, name="xs", tag="xs", align_bytes=64)
-        bs = []
+        xc = keep.tile([P, 8, 4, 256], U32, name="xc", tag="xc", align_bytes=64)
+        xs = keep.tile([P, 8, 4, 256], U8, name="xs", tag="xs", align_bytes=64)
         o0 = []
-        for mt in range(4):
-            bs_t = keep.tile([P, 1024], F32, name="bs%d" % mt, tag="bs%d" % mt)
-            o0_t = keep.tile([P, 1024], F32, name="o0%d" % mt, tag="o0%d" % mt)
-            bs.append(bs_t)
+        for t in range(4):
+            o0_t = keep.tile([P, 1024], F32, name="o0%d" % t, tag="o0%d" % t)
             o0.append(o0_t)
 
         ctx.enter_context(tc.manual_schedule())
@@ -72,267 +71,232 @@ def tile_gemmrstritonpcie_kernel(tc, x, weight, bias, out_0, out_1):
         nc.scalar.activation(out=warm[:], in_=zeros[:], func=ACT.Identity,
                              bias=zeros[:, 0:1], scale=zeros[:, 0:1])
 
-        runs = []
-        for s in range(NE):
-            for op in ("x", "w"):
-                runs.append([(op, 0, 2 * s + a, (op, 0, s), a) for a in range(2)])
-        for g in range(2 * NE, 16):
-            runs.append([("x", 0, g, ("x", 0, g // 2), g % 2), ("w", 0, g, ("w", 0, g // 2), g % 2)])
-        for s in range(8):
-            runs.append([("w", 1, 2 * s + a, ("w", 1, s), a) for a in range(2)])
-        load_seq = []
-        for s in range(8):
-            load_seq.append(("x", 0, s))
-            load_seq.append(("w", 0, s))
-        for s in range(8):
-            load_seq.append(("w", 1, s))
-
-        def last_use(j):
-            if j < 2 * NE:
-                return j
-            return 2 * (j // 2) + 1 if j < 16 else j
+        tiles = []
+        for r in range(4):
+            tiles.extend([("w", 0, r, 0), ("w", 0, r, 1), ("x", 0, r, 0), ("x", 0, r, 1)])
+        for r in range(4):
+            tiles.extend([("w", 1, r, 0), ("w", 1, r, 1)])
 
         raws = {}
         pres = {}
+        gws = {}
+        gxs = {}
         wcodes = {}
         braws = {}
         accs = {}
         tsum = {}
-        state = {"next_load": 0}
 
-        def dram_rows(key, ks):
-            op, half, stage = key
-            rank = stage // 2
+        out0_rows = out_0.flatten_outer_dims().rearrange("(p t) n -> p t n", t=4)
+        out1_rows = out_1.flatten_outer_dims().rearrange("(p t) n -> p t n", t=4)
+        bias_rows = bias.rearrange("r (p t) n -> p t r n", t=4)
+
+        def load(i):
+            op, half, r, pair = tiles[i]
             if op == "x":
-                src = x[rank, :, ks]
+                src = x[r]
             else:
-                src = weight[rank, 512 * half:512 * (half + 1), ks]
-            return src.rearrange("(t p) k -> p t k", p=P)
+                src = weight[r, 512 * half:512 * (half + 1), :]
+            raw = rawp.tile([P, 2, 2048], BF16, name="raw", tag="raw")
+            nc.sync.dma_start(out=raw[:], in_=src.rearrange("(p t) k -> p t k", t=4)[:, 2 * pair:2 * pair + 2, :])
+            raws[i] = raw
 
-        def load_whole(key):
-            k0 = 1024 * (key[2] % 2)
-            raw = rawp.tile([P, 4, 1024], BF16, name="raw", tag="raw")
-            nc.sync.dma_start(out=raw[:], in_=dram_rows(key, slice(k0, k0 + 1024)))
-            raws[key] = (raw, False)
-
-        def load_pieces(key, cuts):
-            k0 = 1024 * (key[2] % 2)
-            raw = rawp.tile([P, 4, 1024], BF16, name="raw", tag="raw")
-            src = dram_rows(key, slice(k0, k0 + 1024))
-            for t0, t1 in cuts:
-                nc.sync.dma_start(out=raw[:, t0:t1, :], in_=src[:, t0:t1, :])
-            raws[key] = (raw, False)
-
-        def free_slot(j, i):
-            return j < NB_RAW or last_use(j - NB_RAW) <= i - 1
-
-        def emit_loads(i):
-            while state["next_load"] < NRUN and free_slot(state["next_load"], i):
-                j = state["next_load"]
-                if j == 0:
-                    load_pieces(load_seq[j], [(0, 1), (1, 2), (2, 4)])
-                elif j < 2 * NE:
-                    load_pieces(load_seq[j], [(0, 2), (2, 4)])
-                else:
-                    load_whole(load_seq[j])
-                state["next_load"] = j + 1
-
-        def unit_words(unit, t0, nt):
-            raw, split = raws[unit[3]]
-            a = unit[4]
-            if split:
-                return raw[:, a, t0:t0 + nt, :].bitcast(F32)
-            return raw[:, t0:t0 + nt, 512 * a:512 * (a + 1)].bitcast(F32)
-
-        def pre_tile(unit):
-            uid = unit[0:3]
-            if uid not in pres:
-                pt = prep.tile([P, 4, 2, P], F32, name="pt", tag="pt")
-                pres[uid] = pt
-            return pres[uid]
-
-        def pre_piece(unit, t0, nt, eng):
-            pt = pre_tile(unit)
-            src = unit_words(unit, t0, nt).rearrange("p t (w u) -> p t u w", u=2)
+        def pre_piece(i, a0, a1, eng):
+            if i not in pres:
+                pt = prep.tile([P, 2, 4, 2, P], F32, name="pt", tag="pt")
+                pres[i] = pt
+            src = raws[i][:].bitcast(F32).rearrange("p t (a w u) -> p t a u w", a=4, u=2)
             if eng == "V":
-                nc.vector.tensor_copy(out=pt[:, t0:t0 + nt, :, :], in_=src)
+                nc.vector.tensor_copy(out=pres[i][:, :, a0:a1], in_=src[:, :, a0:a1])
             else:
-                nc.scalar.copy(out=pt[:, t0:t0 + nt, :, :], in_=src)
+                nc.scalar.copy(out=pres[i][:, :, a0:a1], in_=src[:, :, a0:a1])
 
-        def pre_vector(j, which):
-            if j >= NRUN:
-                return
-            pat = pre_pattern(j)
-            tps = [tp for tp in range(2) if pat[2 * which + tp] == "V"]
-            if tps:
-                pre_piece(runs[j][which], 2 * tps[0], 2 * len(tps), "V")
+        def pre_vector(i):
+            if i < NT and shares(i)[0] > 0:
+                pre_piece(i, 0, shares(i)[0], "V")
 
-        def pre_scalar_list(j):
-            if j >= NRUN:
-                return []
-            pat = pre_pattern(j)
-            return [(runs[j][k // 2], k % 2) for k in range(4) if pat[k] == "S"]
+        def pre_scalar(i, part):
+            if i < NT and part < shares(i)[1]:
+                a = shares(i)[0] + part
+                pre_piece(i, a, a + 1, "S")
 
-        def bank(i, k, g):
-            unit = runs[i][k // 2]
-            tp = k % 2
+        def bank(i, a):
+            op, half, r, pair = tiles[i]
+            if op == "x":
+                if i not in gxs:
+                    g = gxp.tile([P, 4, 1024], BF16, name="gx", tag="gx", align_bytes=64)
+                    gxs[i] = g
+                dst = gxs[i][:].bitcast(F32)[:, a, :]
+            else:
+                if (half, r) not in gws:
+                    g = gwp.tile([P, 4, 2048], BF16, name="gw", tag="gw", align_bytes=64)
+                    gws[(half, r)] = g
+                dst = gws[(half, r)][:].bitcast(F32)[:, a, 512 * pair:512 * (pair + 1)]
             tr = trp.tile([P, 2, 2, P], F32, name="tr", tag="tr")
             for tt in range(2):
                 for u in range(2):
-                    if pre_pattern(i)[k] == "-":
-                        src = unit_words(unit, 2 * tp + tt, 1)[:, 0, u:256:2]
+                    if a < shares(i)[0] + shares(i)[1]:
+                        src = pres[i][:, tt, a, u, :]
                     else:
-                        src = pres[unit[0:3]][:, 2 * tp + tt, u, :]
+                        src = raws[i][:, tt, 512 * a:512 * (a + 1)].bitcast(F32)[:, u:256:2]
                     nc.tensor.transpose(tr[:, tt, u, :], src, ident[:])
-            gw = g[:].bitcast(F32)
-            nc.scalar.copy(
-                out=gw[:, 512 * tp:512 * (tp + 1)].rearrange("p (tt r u) -> p tt r u", tt=2, u=2),
-                in_=tr[:].rearrange("p tt u r -> p tt r u"),
-            )
+            nc.scalar.copy(out=dst.rearrange("p (tt r u) -> p tt r u", tt=2, u=2),
+                           in_=tr[:].rearrange("p tt u r -> p tt r u"))
 
-        def quantize(unit, g):
-            op, half, g_pass = unit[0:3]
-            if op == "x":
-                codes = xc[:, g_pass, :]
-                scl = xs[:, g_pass, :]
-            else:
-                wc = wcp.tile([P, 512], U32, name="wc", tag="wc", align_bytes=64)
-                ws = wcp.tile([P, 512], U8, name="ws", tag="ws", align_bytes=64)
-                wcodes[(half, g_pass)] = (wc, ws)
-                codes = wc[:]
-                scl = ws[:]
-            nc.vector.quantize_mx(out=codes.bitcast(FP8X4), scales=scl, in_=g[:])
+        def quantize_x(i):
+            op, half, r, pair = tiles[i]
+            nc.vector.quantize_mx(out=xc[:, 2 * r + pair].rearrange("p a c -> p (a c)").bitcast(FP8X4),
+                                  scales=xs[:, 2 * r + pair].rearrange("p a c -> p (a c)"),
+                                  in_=gxs[i][:].rearrange("p a c -> p (a c)"))
 
-        def mm(half, g_pass, mt):
-            wc, ws = wcodes[(half, g_pass)]
+        def quantize_w(half, r, a0):
+            if (half, r) not in wcodes:
+                wc = wcp.tile([P, 4, 512], U32, name="wc", tag="wc", align_bytes=64)
+                ws = wcp.tile([P, 4, 512], U8, name="ws", tag="ws", align_bytes=64)
+                wcodes[(half, r)] = (wc, ws)
+            wc, ws = wcodes[(half, r)]
+            nc.vector.quantize_mx(out=wc[:, a0:a0 + 2, :].rearrange("p a c -> p (a c)").bitcast(FP8X4),
+                                  scales=ws[:, a0:a0 + 2, :].rearrange("p a c -> p (a c)"),
+                                  in_=gws[(half, r)][:, a0:a0 + 2, :].rearrange("p a c -> p (a c)"))
+
+        def mm(half, g_pass, t):
+            r = g_pass // 4
+            a = g_pass % 4
+            wc, ws = wcodes[(half, r)]
+            cs = slice(P * (t % 2), P * (t % 2 + 1))
             nc.tensor.matmul_mx(
-                out=accs[(half, mt)][:],
-                lhsT=xc[:, g_pass, P * mt:P * (mt + 1)].bitcast(FP8X4),
-                lhsT_scale=xs[:, g_pass, P * mt:P * (mt + 1)],
-                rhs=wc[:].bitcast(FP8X4),
-                rhs_scale=ws[:],
+                out=accs[(half, t)][:],
+                lhsT=xc[:, 2 * r + t // 2, a, cs].bitcast(FP8X4),
+                lhsT_scale=xs[:, 2 * r + t // 2, a, cs],
+                rhs=wc[:, a, :].bitcast(FP8X4),
+                rhs_scale=ws[:, a, :],
                 start=(g_pass == 0),
                 stop=(g_pass == 15),
             )
 
-        def alloc_acc(half):
-            for mt in range(4):
-                acc = accp.tile([P, 512], F32, name="acc%d" % mt, tag="acc%d" % mt)
-                accs[(half, mt)] = acc
+        def alloc_acc(half, t):
+            acc = accp.tile([P, 512], F32, name="acc%d" % t, tag="acc%d" % t)
+            accs[(half, t)] = acc
 
-        def bias_load(mt, half):
+        def bias_load(t, half):
             braw = bp.tile([P, 4, 512], BF16, name="braw", tag="braw")
-            nc.sync.dma_start(out=braw[:], in_=bias[:, P * mt:P * (mt + 1), 512 * half:512 * (half + 1)]
-                              .rearrange("r p n -> p r n"))
-            braws[(mt, half)] = braw
+            nc.sync.dma_start(out=braw[:], in_=bias_rows[:, t, :, 512 * half:512 * (half + 1)])
+            braws[(t, half)] = braw
 
-        def bias_sum(mt, half, part):
-            braw = braws[(mt, half)]
+        def bias_sum(t, half, part):
+            braw = braws[(t, half)]
             if part == 0:
                 t01 = tmp.tile([P, 512], F32, name="t01", tag="t01")
                 nc.vector.tensor_tensor(out=t01[:], in0=braw[:, 0, :], in1=braw[:, 1, :], op=ALU.add)
-                tsum[(mt, half, 0)] = t01
+                tsum[(t, half, 0)] = t01
             elif part == 1:
                 t23 = tmp.tile([P, 512], F32, name="t23", tag="t23")
                 nc.vector.tensor_tensor(out=t23[:], in0=braw[:, 2, :], in1=braw[:, 3, :], op=ALU.add)
-                tsum[(mt, half, 1)] = t23
+                tsum[(t, half, 1)] = t23
             else:
-                nc.vector.tensor_tensor(out=bs[mt][:, 512 * half:512 * (half + 1)],
-                                        in0=tsum[(mt, half, 0)][:], in1=tsum[(mt, half, 1)][:], op=ALU.add)
+                nc.vector.tensor_tensor(out=o0[t][:, 512 * half:512 * (half + 1)],
+                                        in0=tsum[(t, half, 0)][:], in1=tsum[(t, half, 1)][:], op=ALU.add)
 
-        def ev_add(half, mt):
-            cs = slice(512 * half, 512 * (half + 1))
-            nc.vector.tensor_tensor(out=o0[mt][:, cs], in0=accs[(half, mt)][:], in1=bs[mt][:, cs], op=ALU.add)
+        def ev_add(half, t):
+            o = o0[t][:, 512 * half:512 * (half + 1)].rearrange("p (q s) -> p q s", s=4)
+            nc.vector.tensor_tensor(out=o, in0=accs[(half, t)][:].rearrange("p (s q) -> p q s", s=4), in1=o, op=ALU.add)
 
-        def store0(half, mt):
+        def store0(half, t):
             cs = slice(512 * half, 512 * (half + 1))
-            nc.sync.dma_start(out=out_0[mt, :, cs], in_=o0[mt][:, cs])
+            nc.sync.dma_start(out=out0_rows[:, t, cs], in_=o0[t][:, cs])
 
-        def ev_red(half, mt):
+        def ev_red(half, t):
             cs = slice(512 * half, 512 * (half + 1))
-            nc.vector.tensor_reduce(out=st[:, 2 * mt + half:2 * mt + half + 1], in_=o0[mt][:, cs],
+            nc.vector.tensor_reduce(out=st[:, 2 * t + half:2 * t + half + 1], in_=o0[t][:, cs],
                                     axis=AX.X, op=ALU.max, apply_absolute_value=True)
 
-        def factor(mt):
-            nc.vector.tensor_scalar(out=sc[:, mt:mt + 1], in0=st[:, 2 * mt:2 * mt + 1],
-                                    scalar1=st[:, 2 * mt + 1:2 * mt + 2], scalar2=1.0 / 448.0,
+        def factor(t):
+            nc.vector.tensor_scalar(out=sc[:, t:t + 1], in0=st[:, 2 * t:2 * t + 1],
+                                    scalar1=st[:, 2 * t + 1:2 * t + 2], scalar2=1.0 / 448.0,
                                     op0=ALU.max, op1=ALU.mult)
-            nc.vector.reciprocal(out=fac[:, mt:mt + 1], in_=sc[:, mt:mt + 1])
+            nc.vector.reciprocal(out=fac[:, t:t + 1], in_=sc[:, t:t + 1])
 
-        def cast_store(mt, vcols):
+        def cast_store(t, vcols):
             o1 = o1p.tile([P, 1024], FP8, name="o1", tag="o1")
             if vcols > 0:
-                nc.vector.tensor_scalar(out=o1[:, 0:vcols], in0=o0[mt][:, 0:vcols],
-                                        scalar1=fac[:, mt:mt + 1], scalar2=None, op0=ALU.mult,
+                nc.vector.tensor_scalar(out=o1[:, 0:vcols], in0=o0[t][:, 0:vcols],
+                                        scalar1=fac[:, t:t + 1], scalar2=None, op0=ALU.mult,
                                         saturate=False)
-            nc.scalar.activation(out=o1[:, vcols:1024], in_=o0[mt][:, vcols:1024], func=ACT.Identity,
-                                 bias=zeros[:, 0:1], scale=fac[:, mt:mt + 1], saturate=False)
-            nc.sync.dma_start(out=out_1[mt], in_=o1[:].bitcast(U8))
+            nc.scalar.activation(out=o1[:, vcols:1024], in_=o0[t][:, vcols:1024], func=ACT.Identity,
+                                 bias=zeros[:, 0:1], scale=fac[:, t:t + 1], saturate=False)
+            nc.sync.dma_start(out=out1_rows[:, t, :], in_=o1[:].bitcast(U8))
+
+        mm_plan = {}
+        for r in range(3):
+            for t in range(4):
+                mm_plan[4 * r + 4 + t] = [(0, 4 * r + a, t) for a in range(4)]
+        mm_plan[16] = [(0, 12 + a, t) for t in (0, 1) for a in range(4)]
+        mm_plan[17] = [(0, 12 + a, t) for t in (2, 3) for a in range(4)]
+        for n in range(5):
+            mm_plan[18 + n] = [(1, 2 * n + a, t) for a in range(2) for t in range(4)]
+        mm_plan[23] = [(1, 10 + a, t) for t in (0, 1) for a in range(2)]
+        ev_plan = {16: (0, 1), 17: (2, 3)}
+        red_plan = {18: 0, 19: 1, 20: 2, 21: 3}
+        STORE_STEP = 21
 
         v_extra = {}
-        todo = [(mt, 0, part) for mt in range(4) for part in range(3)]
+        todo = [(t, 0, part) for t in range(4) for part in range(3)]
         for n, item in enumerate(todo):
-            v_extra.setdefault(4 + n, []).append(item)
-        todo = [(mt, 1, part) for mt in range(4) for part in range(3)]
+            v_extra.setdefault(B0_START + n * 11 // 12, []).append(item)
+        todo = [(t, 1, part) for t in range(4) for part in range(3)]
         for n, item in enumerate(todo):
-            v_extra.setdefault(17 + n // 2, []).append(item)
+            v_extra.setdefault(B1_START + n // 2, []).append(item)
         b_load = {}
         for step in sorted(v_extra):
-            for mt, half, part in v_extra[step]:
+            for t, half, part in v_extra[step]:
                 if part == 0:
-                    b_load.setdefault(step - 2, []).append((mt, half))
+                    b_load.setdefault(step - B_LEAD, []).append((t, half))
 
-        emit_loads(0)
-        alloc_acc(0)
-        for j in range(PA):
-            pre_vector(j, 0)
-            pre_vector(j, 1)
-        for i in range(NRUN):
+        state = {"next_load": 0}
+
+        def emit_loads(i):
+            while state["next_load"] < NT and state["next_load"] < i + NB_RAW - 1:
+                load(state["next_load"])
+                state["next_load"] = state["next_load"] + 1
+
+        for t in range(4):
+            alloc_acc(0, t)
+        for i in range(NT + 1):
             emit_loads(i)
-            for mt, half in b_load.get(i, []):
-                bias_load(mt, half)
-            j = i + PA
-            s_list = pre_scalar_list(j)
-            pre_vector(j, 0)
-            g0 = grp.tile([P, 2048], BF16, name="g", tag="g", align_bytes=64)
-            g1 = grp.tile([P, 2048], BF16, name="g", tag="g", align_bytes=64)
-            gs = [g0, g1]
-            for k in ((0, 2, 1, 3) if i < 2 * NE else (0, 1, 2, 3)):
-                bank(i, k, gs[k // 2])
-                if s_list:
-                    unit, tp = s_list[0]
-                    s_list = s_list[1:]
-                    pre_piece(unit, 2 * tp, 2, "S")
-            if LAG <= i < FIRST2:
-                for mt in range(4):
-                    mm(0, i - LAG, mt)
-            elif FIRST2 <= i < TAIL_STEP:
-                if i == FIRST2:
-                    alloc_acc(1)
-                for g_pass in (2 * (i - FIRST2), 2 * (i - FIRST2) + 1):
-                    for mt in range(4):
-                        mm(1, g_pass, mt)
-            quantize(runs[i][0], g0)
-            pre_vector(j, 1)
-            if i == FIRST2 - 1:
-                for mt in range(4):
-                    ev_add(0, mt)
-            quantize(runs[i][1], g1)
-            if i == FIRST2 - 1:
-                for mt in range(4):
-                    store0(0, mt)
-            if FIRST2 <= i < FIRST2 + 4:
-                ev_red(0, i - FIRST2)
-            for mt, half, part in v_extra.get(i, []):
-                bias_sum(mt, half, part)
+            for t, half in b_load.get(i, []):
+                bias_load(t, half)
+            pre_vector(i + PA)
+            if i >= 1:
+                op, half, r, pair = tiles[i - 1]
+                if op == "x":
+                    quantize_x(i - 1)
+                elif pair == 1:
+                    quantize_w(half, r, 2)
+            if i < NT:
+                for a in range(4):
+                    bank(i, a)
+                    pre_scalar(i + PA, a)
+            for half, g_pass, t in mm_plan.get(i, []):
+                if (half, t) not in accs:
+                    alloc_acc(half, t)
+                mm(half, g_pass, t)
+            for t in ev_plan.get(i, ()):
+                ev_add(0, t)
+            for t, half, part in v_extra.get(i, []):
+                bias_sum(t, half, part)
+            if i == STORE_STEP:
+                for t in range(4):
+                    store0(0, t)
+            if i in red_plan:
+                ev_red(0, red_plan[i])
+            if i < NT:
+                op, half, r, pair = tiles[i]
+                if op == "w" and pair == 1:
+                    quantize_w(half, r, 0)
 
-        d = 2 * (TAIL_STEP - FIRST2)
-        for mt in (0, 1):
-            for g_pass in range(d, 14):
-                mm(1, g_pass, mt)
-        for mt in (0, 1):
-            for g_pass in range(14, 16):
-                mm(1, g_pass, mt)
+        for first in (12, 14):
+            for t in (0, 1):
+                for g_pass in (first, first + 1):
+                    mm(1, g_pass, t)
         ev_add(1, 0)
         store0(1, 0)
         ev_add(1, 1)
@@ -343,11 +307,11 @@ def tile_gemmrstritonpcie_kernel(tc, x, weight, bias, out_0, out_1):
         cast_store(0, 0)
         factor(1)
         cast_store(1, 0)
-        for mt in (2, 3):
-            for g_pass in range(d, 16):
-                mm(1, g_pass, mt)
-            ev_add(1, mt)
-            store0(1, mt)
-            ev_red(1, mt)
-            factor(mt)
-            cast_store(mt, 0 if mt == 2 else 640)
+        for t in (2, 3):
+            for g_pass in range(10, 16):
+                mm(1, g_pass, t)
+            ev_add(1, t)
+            store0(1, t)
+            ev_red(1, t)
+            factor(t)
+            cast_store(t, 0 if t == 2 else 640)

@@ -31,6 +31,8 @@ def shares(i):
         return (0, 0)
     if i < 16:
         return (3, 0)
+    if i == 16:
+        return (4, 0)
     return (2, 2)
 
 
@@ -279,19 +281,19 @@ def tile_gemmrstritonpcie_kernel(tc, x, weight, bias, out_0, out_1):
                 if (half, t) not in accs:
                     alloc_acc(half, t)
                 mm(half, g_pass, t)
-            for t in ev_plan.get(i, ()):
-                ev_add(0, t)
             for t, half, part in v_extra.get(i, []):
                 bias_sum(t, half, part)
+            if i < NT:
+                op, half, r, pair = tiles[i]
+                if op == "w" and pair == 1:
+                    quantize_w(half, r, 0)
+            for t in ev_plan.get(i, ()):
+                ev_add(0, t)
             if i == STORE_STEP:
                 for t in range(4):
                     store0(0, t)
             if i in red_plan:
                 ev_red(0, red_plan[i])
-            if i < NT:
-                op, half, r, pair = tiles[i]
-                if op == "w" and pair == 1:
-                    quantize_w(half, r, 0)
 
         for first in (12, 14):
             for t in (0, 1):

@@ -18,7 +18,7 @@ AX = mybir.AxisListType
 P = 128
 NT = 24
 NB_RAW = 6
-NB_PRE = 3
+NB_PRE = 2
 NPLAIN = 5
 PA = 1
 B0_START = 5
@@ -45,7 +45,7 @@ def tile_gemmrstritonpcie_kernel(tc, x, weight, bias, out_0, out_1):
         prep = ctx.enter_context(tc.tile_pool(name="prep", bufs=NB_PRE))
         gwp = ctx.enter_context(tc.tile_pool(name="gwp", bufs=2))
         gxp = ctx.enter_context(tc.tile_pool(name="gxp", bufs=2))
-        wcp = ctx.enter_context(tc.tile_pool(name="wcp", bufs=3))
+        wcp = ctx.enter_context(tc.tile_pool(name="wcp", bufs=4))
         bp = ctx.enter_context(tc.tile_pool(name="bp", bufs=4))
         tmp = ctx.enter_context(tc.tile_pool(name="tmp", bufs=2))
         o1p = ctx.enter_context(tc.tile_pool(name="o1p", bufs=4))
@@ -233,9 +233,14 @@ def tile_gemmrstritonpcie_kernel(tc, x, weight, bias, out_0, out_1):
                 mm_plan[4 * r + 4 + t] = [(0, 4 * r + a, t) for a in range(4)]
         mm_plan[16] = [(0, 12 + a, t) for t in (0, 1) for a in range(4)]
         mm_plan[17] = [(0, 12 + a, t) for t in (2, 3) for a in range(4)]
-        for n in range(5):
-            mm_plan[18 + n] = [(1, 2 * n + a, t) for a in range(2) for t in range(4)]
-        mm_plan[23] = [(1, 10 + a, t) for t in (0, 1) for a in range(2)]
+        done = [0, 0, 0, 0]
+        for n in range(6):
+            mm_plan[18 + n] = []
+            for a in range(2):
+                for t in range(4):
+                    if a == 0 or t < 2 or n < 2:
+                        mm_plan[18 + n].append((1, done[t], t))
+                        done[t] = done[t] + 1
         ev_plan = {16: (0, 1), 17: (2, 3)}
         red_plan = {18: 0, 19: 1, 20: 2, 21: 3}
         STORE_STEP = 21
@@ -295,10 +300,11 @@ def tile_gemmrstritonpcie_kernel(tc, x, weight, bias, out_0, out_1):
             if i in red_plan:
                 ev_red(0, red_plan[i])
 
-        for first in (12, 14):
+        for upto in (14, 16):
             for t in (0, 1):
-                for g_pass in (first, first + 1):
+                for g_pass in range(done[t], upto):
                     mm(1, g_pass, t)
+                done[t] = upto
         ev_add(1, 0)
         store0(1, 0)
         ev_add(1, 1)
@@ -310,7 +316,7 @@ def tile_gemmrstritonpcie_kernel(tc, x, weight, bias, out_0, out_1):
         factor(1)
         cast_store(1, 0)
         for t in (2, 3):
-            for g_pass in range(10, 16):
+            for g_pass in range(done[t], 16):
                 mm(1, g_pass, t)
             ev_add(1, t)
             store0(1, t)

@@ -21,19 +21,16 @@ NB_RAW = 6
 NB_PRE = 2
 NPLAIN = 5
 PA = 1
-B0_START = 5
-B1_START = 18
-B_LEAD = 3
+BIAS_LOADS = {8: 0, 11: 1, 16: 2, 18: 3}
+BIAS_START = 16
 
 
 def shares(i):
     if i < NPLAIN:
         return (0, 0)
-    if i < 16:
-        return (3, 0)
-    if i == 16:
+    if i < 17:
         return (4, 0)
-    return (2, 2)
+    return (1, 2)
 
 
 def tile_gemmrstritonpcie_kernel(tc, x, weight, bias, out_0, out_1):
@@ -46,8 +43,7 @@ def tile_gemmrstritonpcie_kernel(tc, x, weight, bias, out_0, out_1):
         gwp = ctx.enter_context(tc.tile_pool(name="gwp", bufs=2))
         gxp = ctx.enter_context(tc.tile_pool(name="gxp", bufs=2))
         wcp = ctx.enter_context(tc.tile_pool(name="wcp", bufs=4))
-        bp = ctx.enter_context(tc.tile_pool(name="bp", bufs=4))
-        tmp = ctx.enter_context(tc.tile_pool(name="tmp", bufs=2))
+        bp = ctx.enter_context(tc.tile_pool(name="bp", bufs=3))
         o1p = ctx.enter_context(tc.tile_pool(name="o1p", bufs=4))
         trp = ctx.enter_context(tc.psum_pool(name="trp", bufs=4))
         accp = ctx.enter_context(tc.psum_pool(name="accp", bufs=1))
@@ -63,10 +59,7 @@ def tile_gemmrstritonpcie_kernel(tc, x, weight, bias, out_0, out_1):
 
         xc = keep.tile([P, 8, 4, 256], U32, name="xc", tag="xc", align_bytes=64)
         xs = keep.tile([P, 8, 4, 256], U8, name="xs", tag="xs", align_bytes=64)
-        o0 = []
-        for t in range(4):
-            o0_t = keep.tile([P, 1024], F32, name="o0%d" % t, tag="o0%d" % t)
-            o0.append(o0_t)
+        o0 = keep.tile([P, 4, 1024], F32, name="o0", tag="o0")
 
         ctx.enter_context(tc.manual_schedule())
 
@@ -86,11 +79,10 @@ def tile_gemmrstritonpcie_kernel(tc, x, weight, bias, out_0, out_1):
         wcodes = {}
         braws = {}
         accs = {}
-        tsum = {}
 
         out0_rows = out_0.flatten_outer_dims().rearrange("(p t) n -> p t n", t=4)
         out1_rows = out_1.flatten_outer_dims().rearrange("(p t) n -> p t n", t=4)
-        bias_rows = bias.rearrange("r (p t) n -> p t r n", t=4)
+        bias_rows = bias.rearrange("r (p t) n -> r p t n", t=4)
 
         def load(i):
             op, half, r, pair = tiles[i]
@@ -179,36 +171,33 @@ def tile_gemmrstritonpcie_kernel(tc, x, weight, bias, out_0, out_1):
             acc = accp.tile([P, 512], F32, name="acc%d" % t, tag="acc%d" % t)
             accs[(half, t)] = acc
 
-        def bias_load(t, half):
-            braw = bp.tile([P, 4, 512], BF16, name="braw", tag="braw")
-            nc.sync.dma_start(out=braw[:], in_=bias_rows[:, t, :, 512 * half:512 * (half + 1)])
-            braws[(t, half)] = braw
+        def bias_load(r):
+            braw = bp.tile([P, 4, 1024], BF16, name="braw", tag="braw")
+            nc.sync.dma_start(out=braw[:], in_=bias_rows[r])
+            braws[r] = braw
 
-        def bias_sum(t, half, part):
-            braw = braws[(t, half)]
-            if part == 0:
-                t01 = tmp.tile([P, 512], F32, name="t01", tag="t01")
-                nc.vector.tensor_tensor(out=t01[:], in0=braw[:, 0, :], in1=braw[:, 1, :], op=ALU.add)
-                tsum[(t, half, 0)] = t01
-            elif part == 1:
-                t23 = tmp.tile([P, 512], F32, name="t23", tag="t23")
-                nc.vector.tensor_tensor(out=t23[:], in0=braw[:, 2, :], in1=braw[:, 3, :], op=ALU.add)
-                tsum[(t, half, 1)] = t23
-            else:
-                nc.vector.tensor_tensor(out=o0[t][:, 512 * half:512 * (half + 1)],
-                                        in0=tsum[(t, half, 0)][:], in1=tsum[(t, half, 1)][:], op=ALU.add)
+        def bias_add(r, t0, t1, half):
+            cs = slice(0, 1024) if half is None else slice(512 * half, 512 * (half + 1))
+            first = braws[0] if (r == 1 and half == 1) else o0
+            nc.vector.tensor_tensor(out=o0[:, t0:t1, cs], in0=first[:, t0:t1, cs],
+                                    in1=braws[r][:, t0:t1, cs], op=ALU.add)
 
         def ev_add(half, t):
-            o = o0[t][:, 512 * half:512 * (half + 1)].rearrange("p (q s) -> p q s", s=4)
-            nc.vector.tensor_tensor(out=o, in0=accs[(half, t)][:].rearrange("p (s q) -> p q s", s=4), in1=o, op=ALU.add)
+            cs = slice(512 * half, 512 * (half + 1))
+            o = o0[:, t, cs].rearrange("p (q s) -> p q s", s=4)
+            if half == 0:
+                more = braws[0][:, t, cs].rearrange("p (q s) -> p q s", s=4)
+            else:
+                more = o
+            nc.vector.tensor_tensor(out=o, in0=accs[(half, t)][:].rearrange("p (s q) -> p q s", s=4), in1=more, op=ALU.add)
 
         def store0(half, t):
             cs = slice(512 * half, 512 * (half + 1))
-            nc.sync.dma_start(out=out0_rows[:, t, cs], in_=o0[t][:, cs])
+            nc.sync.dma_start(out=out0_rows[:, t, cs], in_=o0[:, t, cs])
 
         def ev_red(half, t):
             cs = slice(512 * half, 512 * (half + 1))
-            nc.vector.tensor_reduce(out=st[:, 2 * t + half:2 * t + half + 1], in_=o0[t][:, cs],
+            nc.vector.tensor_reduce(out=st[:, 2 * t + half:2 * t + half + 1], in_=o0[:, t, cs],
                                     axis=AX.X, op=ALU.max, apply_absolute_value=True)
 
         def factor(t):
@@ -220,10 +209,10 @@ def tile_gemmrstritonpcie_kernel(tc, x, weight, bias, out_0, out_1):
         def cast_store(t, vcols):
             o1 = o1p.tile([P, 1024], FP8, name="o1", tag="o1")
             if vcols > 0:
-                nc.vector.tensor_scalar(out=o1[:, 0:vcols], in0=o0[t][:, 0:vcols],
+                nc.vector.tensor_scalar(out=o1[:, 0:vcols], in0=o0[:, t, 0:vcols],
                                         scalar1=fac[:, t:t + 1], scalar2=None, op0=ALU.mult,
                                         saturate=False)
-            nc.scalar.activation(out=o1[:, vcols:1024], in_=o0[t][:, vcols:1024], func=ACT.Identity,
+            nc.scalar.activation(out=o1[:, vcols:1024], in_=o0[:, t, vcols:1024], func=ACT.Identity,
                                  bias=zeros[:, 0:1], scale=fac[:, t:t + 1], saturate=False)
             nc.sync.dma_start(out=out1_rows[:, t, :], in_=o1[:].bitcast(U8))
 
@@ -242,21 +231,13 @@ def tile_gemmrstritonpcie_kernel(tc, x, weight, bias, out_0, out_1):
                         mm_plan[18 + n].append((1, done[t], t))
                         done[t] = done[t] + 1
         ev_plan = {16: (0, 1), 17: (2, 3)}
-        red_plan = {18: 0, 19: 1, 20: 2, 21: 3}
-        STORE_STEP = 21
+        red_plan = {21: (0,), 22: (1,), 24: (2, 3)}
 
-        v_extra = {}
-        todo = [(t, 0, part) for t in range(4) for part in range(3)]
+        todo = [(1, 0, 2, 1), (1, 2, 4, 1), (1, 0, 2, 0), (1, 2, 4, 0)]
+        todo.extend([(r, t, t + 1, None) for r in (2, 3) for t in range(4)])
+        bias_plan = {}
         for n, item in enumerate(todo):
-            v_extra.setdefault(B0_START + n * 11 // 12, []).append(item)
-        todo = [(t, 1, part) for t in range(4) for part in range(3)]
-        for n, item in enumerate(todo):
-            v_extra.setdefault(B1_START + n // 2, []).append(item)
-        b_load = {}
-        for step in sorted(v_extra):
-            for t, half, part in v_extra[step]:
-                if part == 0:
-                    b_load.setdefault(step - B_LEAD, []).append((t, half))
+            bias_plan.setdefault(BIAS_START + (n + 1) // 2, []).append(item)
 
         state = {"next_load": 0}
 
@@ -269,8 +250,8 @@ def tile_gemmrstritonpcie_kernel(tc, x, weight, bias, out_0, out_1):
             alloc_acc(0, t)
         for i in range(NT + 1):
             emit_loads(i)
-            for t, half in b_load.get(i, []):
-                bias_load(t, half)
+            if i in BIAS_LOADS:
+                bias_load(BIAS_LOADS[i])
             pre_vector(i + PA)
             if i >= 1:
                 op, half, r, pair = tiles[i - 1]
@@ -286,19 +267,21 @@ def tile_gemmrstritonpcie_kernel(tc, x, weight, bias, out_0, out_1):
                 if (half, t) not in accs:
                     alloc_acc(half, t)
                 mm(half, g_pass, t)
-            for t, half, part in v_extra.get(i, []):
-                bias_sum(t, half, part)
+            for item in bias_plan.get(i, []):
+                if item[3] != 0:
+                    bias_add(*item)
             if i < NT:
                 op, half, r, pair = tiles[i]
                 if op == "w" and pair == 1:
                     quantize_w(half, r, 0)
             for t in ev_plan.get(i, ()):
                 ev_add(0, t)
-            if i == STORE_STEP:
-                for t in range(4):
-                    store0(0, t)
-            if i in red_plan:
-                ev_red(0, red_plan[i])
+            for item in bias_plan.get(i, []):
+                if item[3] == 0:
+                    bias_add(*item)
+            for t in red_plan.get(i, ()):
+                store0(0, t)
+                ev_red(0, t)
 
         for upto in (14, 16):
             for t in (0, 1):

@@ -21,7 +21,7 @@ NB_RAW = 6
 NB_PRE = 2
 NPLAIN = 5
 PA = 1
-BIAS_LOADS = {8: 0, 11: 1, 16: 2, 18: 3}
+BIAS_LOADS = {11: 0, 13: 1, 16: 2, 19: 3}
 BIAS_START = 16
 
 
@@ -30,6 +30,10 @@ def shares(i):
         return (0, 0)
     if i < 17:
         return (4, 0)
+    if i < 19:
+        return (2, 2)
+    if i < 23:
+        return (0, 3 if i < 21 else 2)
     return (1, 2)
 
 
@@ -200,10 +204,12 @@ def tile_gemmrstritonpcie_kernel(tc, x, weight, bias, out_0, out_1):
             nc.vector.tensor_reduce(out=st[:, 2 * t + half:2 * t + half + 1], in_=o0[:, t, cs],
                                     axis=AX.X, op=ALU.max, apply_absolute_value=True)
 
-        def factor(t):
+        def row_scale(t):
             nc.vector.tensor_scalar(out=sc[:, t:t + 1], in0=st[:, 2 * t:2 * t + 1],
                                     scalar1=st[:, 2 * t + 1:2 * t + 2], scalar2=1.0 / 448.0,
                                     op0=ALU.max, op1=ALU.mult)
+
+        def factor(t):
             nc.vector.reciprocal(out=fac[:, t:t + 1], in_=sc[:, t:t + 1])
 
         def cast_store(t, vcols):
@@ -288,21 +294,24 @@ def tile_gemmrstritonpcie_kernel(tc, x, weight, bias, out_0, out_1):
                 for g_pass in range(done[t], upto):
                     mm(1, g_pass, t)
                 done[t] = upto
-        ev_add(1, 0)
-        store0(1, 0)
-        ev_add(1, 1)
-        store0(1, 1)
-        ev_red(1, 0)
-        ev_red(1, 1)
-        factor(0)
-        cast_store(0, 0)
-        factor(1)
-        cast_store(1, 0)
         for t in (2, 3):
             for g_pass in range(done[t], 16):
                 mm(1, g_pass, t)
+        for t in (0, 1):
+            ev_add(1, t)
+            store0(1, t)
+        for t in (0, 1):
+            ev_red(1, t)
+        for t in (0, 1):
+            row_scale(t)
+        for t in (0, 1):
+            factor(t)
+        for t in (0, 1):
+            cast_store(t, 0)
+        for t in (2, 3):
             ev_add(1, t)
             store0(1, t)
             ev_red(1, t)
+            row_scale(t)
             factor(t)
             cast_store(t, 0 if t == 2 else 640)

@@ -22,10 +22,13 @@ NB_PRE = 2
 NPLAIN = 5
 PA = 1
 BIAS_LOADS = {11: 0, 13: 1, 16: 2, 19: 3}
+FIRST_COUNTS = (3, 3, 4, 4, 2)
 BIAS_START = 16
 
 
 def shares(i):
+    if i == 4:
+        return (2, 0)
     if i < NPLAIN:
         return (0, 0)
     if i < 17:
@@ -71,7 +74,8 @@ def tile_gemmrstritonpcie_kernel(tc, x, weight, bias, out_0, out_1):
                              bias=zeros[:, 0:1], scale=zeros[:, 0:1])
 
         tiles = []
-        for r in range(4):
+        tiles.extend([("x", 0, 0, 0), ("w", 0, 0, 0), ("w", 0, 0, 1), ("x", 0, 0, 1)])
+        for r in range(1, 4):
             tiles.extend([("w", 0, r, 0), ("w", 0, r, 1), ("x", 0, r, 0), ("x", 0, r, 1)])
         for r in range(4):
             tiles.extend([("w", 1, r, 0), ("w", 1, r, 1)])
@@ -223,9 +227,16 @@ def tile_gemmrstritonpcie_kernel(tc, x, weight, bias, out_0, out_1):
             nc.sync.dma_start(out=out1_rows[:, t, :], in_=o1[:].bitcast(U8))
 
         mm_plan = {}
-        for r in range(3):
+        first = []
+        for ts in ((0, 1), (2, 3)):
+            for a0 in (0, 2):
+                first.extend([(0, a0 + a, t) for t in ts for a in range(2)])
+        for n, count in enumerate(FIRST_COUNTS):
+            mm_plan[3 + n] = first[:count]
+            first = first[count:]
+        for r in range(1, 3):
             for t in range(4):
-                mm_plan[4 * r + 4 + t] = [(0, 4 * r + a, t) for a in range(4)]
+                mm_plan.setdefault(4 * r + 4 + t, []).extend([(0, 4 * r + a, t) for a in range(4)])
         mm_plan[16] = [(0, 12 + a, t) for t in (0, 1) for a in range(4)]
         mm_plan[17] = [(0, 12 + a, t) for t in (2, 3) for a in range(4)]
         done = [0, 0, 0, 0]
@@ -304,14 +315,19 @@ def tile_gemmrstritonpcie_kernel(tc, x, weight, bias, out_0, out_1):
             ev_red(1, t)
         for t in (0, 1):
             row_scale(t)
-        for t in (0, 1):
-            factor(t)
-        for t in (0, 1):
-            cast_store(t, 0)
-        for t in (2, 3):
-            ev_add(1, t)
-            store0(1, t)
-            ev_red(1, t)
-            row_scale(t)
-            factor(t)
-            cast_store(t, 0 if t == 2 else 640)
+        factor(0)
+        cast_store(0, 0)
+        ev_add(1, 2)
+        store0(1, 2)
+        factor(1)
+        cast_store(1, 0)
+        ev_red(1, 2)
+        row_scale(2)
+        ev_add(1, 3)
+        store0(1, 3)
+        factor(2)
+        cast_store(2, 0)
+        ev_red(1, 3)
+        row_scale(3)
+        factor(3)
+        cast_store(3, 640)

@@ -21,9 +21,8 @@ NB_RAW = 6
 NB_PRE = 2
 NPLAIN = 5
 PA = 1
-BIAS_LOADS = {11: 0, 13: 1, 16: 2, 19: 3}
+BIAS_LOADS = {9: 0, 13: 1, 14: 2, 18: 3}
 FIRST_COUNTS = (3, 3, 4, 4, 2)
-BIAS_START = 16
 
 
 def shares(i):
@@ -33,11 +32,9 @@ def shares(i):
         return (0, 0)
     if i < 17:
         return (4, 0)
-    if i < 19:
-        return (2, 2)
-    if i < 23:
-        return (0, 3 if i < 21 else 2)
-    return (1, 2)
+    if 19 <= i < 23:
+        return (0, 2)
+    return (2, 2)
 
 
 def tile_gemmrstritonpcie_kernel(tc, x, weight, bias, out_0, out_1):
@@ -244,17 +241,18 @@ def tile_gemmrstritonpcie_kernel(tc, x, weight, bias, out_0, out_1):
             mm_plan[18 + n] = []
             for a in range(2):
                 for t in range(4):
-                    if a == 0 or t < 2 or n < 2:
+                    if a == 0 or t < 3:
                         mm_plan[18 + n].append((1, done[t], t))
                         done[t] = done[t] + 1
         ev_plan = {16: (0, 1), 17: (2, 3)}
         red_plan = {21: (0,), 22: (1,), 24: (2, 3)}
 
-        todo = [(1, 0, 2, 1), (1, 2, 4, 1), (1, 0, 2, 0), (1, 2, 4, 0)]
-        todo.extend([(r, t, t + 1, None) for r in (2, 3) for t in range(4)])
-        bias_plan = {}
-        for n, item in enumerate(todo):
-            bias_plan.setdefault(BIAS_START + (n + 1) // 2, []).append(item)
+        bias_plan = {
+            16: [(1, 0, 2, 1), (1, 2, 4, 1)],
+            18: [(1, 0, 2, 0), (1, 2, 4, 0)],
+        }
+        for n in range(4):
+            bias_plan[19 + n] = [(2 + n // 2, t, t + 1, None) for t in (2 * (n % 2), 2 * (n % 2) + 1)]
 
         state = {"next_load": 0}
 

@@ -22,7 +22,7 @@ NB_PRE = 2
 NPLAIN = 5
 PA = 1
 BIAS_LOADS = {9: 0, 13: 1, 14: 2, 18: 3}
-FIRST_COUNTS = (3, 3, 4, 4, 2)
+FIRST_COUNTS = (3, 3, 3, 4, 3)
 
 
 def shares(i):
@@ -32,8 +32,10 @@ def shares(i):
         return (0, 0)
     if i < 17:
         return (4, 0)
-    if 19 <= i < 23:
+    if 19 <= i < 22:
         return (0, 2)
+    if i == 22:
+        return (1, 2)
     return (2, 2)
 
 
@@ -277,7 +279,8 @@ def tile_gemmrstritonpcie_kernel(tc, x, weight, bias, out_0, out_1):
             if i < NT:
                 for a in range(4):
                     bank(i, a)
-                    pre_scalar(i + PA, a)
+                    if a > 0:
+                        pre_scalar(i + PA, a - 1)
             for half, g_pass, t in mm_plan.get(i, []):
                 if (half, t) not in accs:
                     alloc_acc(half, t)

@@ -279,8 +279,9 @@ def tile_gemmrstritonpcie_kernel(tc, x, weight, bias, out_0, out_1):
             if i < NT:
                 for a in range(4):
                     bank(i, a)
-                    if a > 0:
-                        pre_scalar(i + PA, a - 1)
+                    if a == 2:
+                        for part in range(shares(i + PA)[1]):
+                            pre_scalar(i + PA, part)
             for half, g_pass, t in mm_plan.get(i, []):
                 if (half, t) not in accs:
                     alloc_acc(half, t)

from contextlib import ExitStack

import concourse.mybir as mybir
from concourse.masks import make_identity

FLOPS = 2 * 512 * 1024 * 8192

F32 = mybir.dt.float32
BF16 = mybir.dt.bfloat16
U32 = mybir.dt.uint32
U8 = mybir.dt.uint8
FP8 = mybir.dt.float8_e4m3fn
FP8X4 = mybir.dt.float8_e4m3fn_x4
ALU = mybir.AluOpType
ACT = mybir.ActivationFunctionType
AX = mybir.AxisListType

P = 128
NT = 24
NB_RAW = 6
NB_PRE = 2
NPLAIN = 5
PA = 1
BIAS_LOADS = {9: 0, 13: 1, 14: 2, 18: 3}
FIRST_COUNTS = (3, 3, 3, 4, 3)


def shares(i):
    if i == 4:
        return (2, 0)
    if i < NPLAIN:
        return (0, 0)
    if i < 17:
        return (4, 0)
    if 19 <= i < 22:
        return (0, 2)
    if i == 22:
        return (1, 2)
    return (2, 2)


def tile_gemmrstritonpcie_kernel(tc, x, weight, bias, out_0, out_1):
    nc = tc.nc
    with ExitStack() as ctx:
        const = ctx.enter_context(tc.tile_pool(name="const", bufs=1))
        keep = ctx.enter_context(tc.tile_pool(name="keep", bufs=1))
        rawp = ctx.enter_context(tc.tile_pool(name="rawp", bufs=NB_RAW))
        prep = ctx.enter_context(tc.tile_pool(name="prep", bufs=NB_PRE))
        gwp = ctx.enter_context(tc.tile_pool(name="gwp", bufs=2))
        gxp = ctx.enter_context(tc.tile_pool(name="gxp", bufs=2))
        wcp = ctx.enter_context(tc.tile_pool(name="wcp", bufs=4))
        bp = ctx.enter_context(tc.tile_pool(name="bp", bufs=3))
        o1p = ctx.enter_context(tc.tile_pool(name="o1p", bufs=4))
        trp = ctx.enter_context(tc.psum_pool(name="trp", bufs=4))
        accp = ctx.enter_context(tc.psum_pool(name="accp", bufs=1))

        ident = const.tile([P, P], F32, name="ident", tag="ident")
        make_identity(nc, ident[:])
        zeros = const.tile([P, 1], F32, name="zeros", tag="zeros")
        nc.vector.memset(zeros[:], 0.0)
        warm = const.tile([P, 1], F32, name="warm", tag="warm")
        st = const.tile([P, 8], F32, name="st", tag="st")
        sc = const.tile([P, 4], F32, name="sc", tag="sc")
        fac = const.tile([P, 4], F32, name="fac", tag="fac")

        xc = keep.tile([P, 8, 4, 256], U32, name="xc", tag="xc", align_bytes=64)
        xs = keep.tile([P, 8, 4, 256], U8, name="xs", tag="xs", align_bytes=64)
        o0 = keep.tile([P, 4, 1024], F32, name="o0", tag="o0")

        ctx.enter_context(tc.manual_schedule())

        nc.scalar.activation(out=warm[:], in_=zeros[:], func=ACT.Identity,
                             bias=zeros[:, 0:1], scale=zeros[:, 0:1])

        tiles = []
        tiles.extend([("x", 0, 0, 0), ("w", 0, 0, 0), ("w", 0, 0, 1), ("x", 0, 0, 1)])
        for r in range(1, 4):
            tiles.extend([("w", 0, r, 0), ("w", 0, r, 1), ("x", 0, r, 0), ("x", 0, r, 1)])
        for r in range(4):
            tiles.extend([("w", 1, r, 0), ("w", 1, r, 1)])

        raws = {}
        pres = {}
        gws = {}
        gxs = {}
        wcodes = {}
        braws = {}
        accs = {}

        out0_rows = out_0.flatten_outer_dims().rearrange("(p t) n -> p t n", t=4)
        out1_rows = out_1.flatten_outer_dims().rearrange("(p t) n -> p t n", t=4)
        bias_rows = bias.rearrange("r (p t) n -> r p t n", t=4)

        def load(i):
            op, half, r, pair = tiles[i]
            if op == "x":
                src = x[r]
            else:
                src = weight[r, 512 * half:512 * (half + 1), :]
            raw = rawp.tile([P, 2, 2048], BF16, name="raw", tag="raw")
            nc.sync.dma_start(out=raw[:], in_=src.rearrange("(p t) k -> p t k", t=4)[:, 2 * pair:2 * pair + 2, :])
            raws[i] = raw

        def pre_piece(i, a0, a1, eng):
            if i not in pres:
                pt = prep.tile([P, 2, 4, 2, P], F32, name="pt", tag="pt")
                pres[i] = pt
            src = raws[i][:].bitcast(F32).rearrange("p t (a w u) -> p t a u w", a=4, u=2)
            if eng == "V":
                nc.vector.tensor_copy(out=pres[i][:, :, a0:a1], in_=src[:, :, a0:a1])
            else:
                nc.scalar.copy(out=pres[i][:, :, a0:a1], in_=src[:, :, a0:a1])

        def pre_vector(i):
            if i < NT and shares(i)[0] > 0:
                pre_piece(i, 0, shares(i)[0], "V")

        def pre_scalar(i, part):
            if i < NT and part < shares(i)[1]:
                a = shares(i)[0] + part
                pre_piece(i, a, a + 1, "S")

        def bank(i, a):
            op, half, r, pair = tiles[i]
            if op == "x":
                if i not in gxs:
                    g = gxp.tile([P, 4, 1024], BF16, name="gx", tag="gx", align_bytes=64)
                    gxs[i] = g
                dst = gxs[i][:].bitcast(F32)[:, a, :]
            else:
                if (half, r) not in gws:
                    g = gwp.tile([P, 4, 2048], BF16, name="gw", tag="gw", align_bytes=64)
                    gws[(half, r)] = g
                dst = gws[(half, r)][:].bitcast(F32)[:, a, 512 * pair:512 * (pair + 1)]
            tr = trp.tile([P, 2, 2, P], F32, name="tr", tag="tr")
            for tt in range(2):
                for u in range(2):
                    if a < shares(i)[0] + shares(i)[1]:
                        src = pres[i][:, tt, a, u, :]
                    else:
                        src = raws[i][:, tt, 512 * a:512 * (a + 1)].bitcast(F32)[:, u:256:2]
                    nc.tensor.transpose(tr[:, tt, u, :], src, ident[:])
            nc.scalar.copy(out=dst.rearrange("p (tt r u) -> p tt r u", tt=2, u=2),
                           in_=tr[:].rearrange("p tt u r -> p tt r u"))

        def quantize_x(i):
            op, half, r, pair = tiles[i]
            nc.vector.quantize_mx(out=xc[:, 2 * r + pair].rearrange("p a c -> p (a c)").bitcast(FP8X4),
                                  scales=xs[:, 2 * r + pair].rearrange("p a c -> p (a c)"),
                                  in_=gxs[i][:].rearrange("p a c -> p (a c)"))

        def quantize_w(half, r, a0):
            if (half, r) not in wcodes:
                wc = wcp.tile([P, 4, 512], U32, name="wc", tag="wc", align_bytes=64)
                ws = wcp.tile([P, 4, 512], U8, name="ws", tag="ws", align_bytes=64)
                wcodes[(half, r)] = (wc, ws)
            wc, ws = wcodes[(half, r)]
            nc.vector.quantize_mx(out=wc[:, a0:a0 + 2, :].rearrange("p a c -> p (a c)").bitcast(FP8X4),
                                  scales=ws[:, a0:a0 + 2, :].rearrange("p a c -> p (a c)"),
                                  in_=gws[(half, r)][:, a0:a0 + 2, :].rearrange("p a c -> p (a c)"))

        def mm(half, g_pass, t):
            r = g_pass // 4
            a = g_pass % 4
            wc, ws = wcodes[(half, r)]
            cs = slice(P * (t % 2), P * (t % 2 + 1))
            nc.tensor.matmul_mx(
                out=accs[(half, t)][:],
                lhsT=xc[:, 2 * r + t // 2, a, cs].bitcast(FP8X4),
                lhsT_scale=xs[:, 2 * r + t // 2, a, cs],
                rhs=wc[:, a, :].bitcast(FP8X4),
                rhs_scale=ws[:, a, :],
                start=(g_pass == 0),
                stop=(g_pass == 15),
            )

        def alloc_acc(half, t):
            acc = accp.tile([P, 512], F32, name="acc%d" % t, tag="acc%d" % t)
            accs[(half, t)] = acc

        def bias_load(r):
            braw = bp.tile([P, 4, 1024], BF16, name="braw", tag="braw")
            nc.sync.dma_start(out=braw[:], in_=bias_rows[r])
            braws[r] = braw

        def bias_add(r, t0, t1, half):
            cs = slice(0, 1024) if half is None else slice(512 * half, 512 * (half + 1))
            first = braws[0] if (r == 1 and half == 1) else o0
            nc.vector.tensor_tensor(out=o0[:, t0:t1, cs], in0=first[:, t0:t1, cs],
                                    in1=braws[r][:, t0:t1, cs], op=ALU.add)

        def ev_add(half, t):
            cs = slice(512 * half, 512 * (half + 1))
            o = o0[:, t, cs].rearrange("p (q s) -> p q s", s=4)
            if half == 0:
                more = braws[0][:, t, cs].rearrange("p (q s) -> p q s", s=4)
            else:
                more = o
            nc.vector.tensor_tensor(out=o, in0=accs[(half, t)][:].rearrange("p (s q) -> p q s", s=4), in1=more, op=ALU.add)

        def store0(half, t):
            cs = slice(512 * half, 512 * (half + 1))
            nc.sync.dma_start(out=out0_rows[:, t, cs], in_=o0[:, t, cs])

        def ev_red(half, t):
            cs = slice(512 * half, 512 * (half + 1))
            nc.vector.tensor_reduce(out=st[:, 2 * t + half:2 * t + half + 1], in_=o0[:, t, cs],
                                    axis=AX.X, op=ALU.max, apply_absolute_value=True)

        def row_scale(t):
            nc.vector.tensor_scalar(out=sc[:, t:t + 1], in0=st[:, 2 * t:2 * t + 1],
                                    scalar1=st[:, 2 * t + 1:2 * t + 2], scalar2=1.0 / 448.0,
                                    op0=ALU.max, op1=ALU.mult)

        def factor(t):
            nc.vector.reciprocal(out=fac[:, t:t + 1], in_=sc[:, t:t + 1])

        def cast_store(t, vcols):
            o1 = o1p.tile([P, 1024], FP8, name="o1", tag="o1")
            if vcols > 0:
                nc.vector.tensor_scalar(out=o1[:, 0:vcols], in0=o0[:, t, 0:vcols],
                                        scalar1=fac[:, t:t + 1], scalar2=None, op0=ALU.mult,
                                        saturate=False)
            nc.scalar.activation(out=o1[:, vcols:1024], in_=o0[:, t, vcols:1024], func=ACT.Identity,
                                 bias=zeros[:, 0:1], scale=fac[:, t:t + 1], saturate=False)
            nc.sync.dma_start(out=out1_rows[:, t, :], in_=o1[:].bitcast(U8))

        mm_plan = {}
        first = []
        for ts in ((0, 1), (2, 3)):
            for a0 in (0, 2):
                first.extend([(0, a0 + a, t) for t in ts for a in range(2)])
        for n, count in enumerate(FIRST_COUNTS):
            mm_plan[3 + n] = first[:count]
            first = first[count:]
        for r in range(1, 3):
            for t in range(4):
                mm_plan.setdefault(4 * r + 4 + t, []).extend([(0, 4 * r + a, t) for a in range(4)])
        mm_plan[16] = [(0, 12 + a, t) for t in (0, 1) for a in range(4)]
        mm_plan[17] = [(0, 12 + a, t) for t in (2, 3) for a in range(4)]
        done = [0, 0, 0, 0]
        for n in range(6):
            mm_plan[18 + n] = []
            for a in range(2):
                for t in range(4):
                    if a == 0 or t < 3:
                        mm_plan[18 + n].append((1, done[t], t))
                        done[t] = done[t] + 1
        ev_plan = {16: (0, 1), 17: (2, 3)}
        red_plan = {21: (0,), 22: (1,), 24: (2, 3)}

        bias_plan = {
            16: [(1, 0, 2, 1), (1, 2, 4, 1)],
            18: [(1, 0, 2, 0), (1, 2, 4, 0)],
        }
        for n in range(4):
            bias_plan[19 + n] = [(2 + n // 2, t, t + 1, None) for t in (2 * (n % 2), 2 * (n % 2) + 1)]

        state = {"next_load": 0}

        def emit_loads(i):
            while state["next_load"] < NT and state["next_load"] < i + NB_RAW - 1:
                load(state["next_load"])
                state["next_load"] = state["next_load"] + 1

        for t in range(4):
            alloc_acc(0, t)
        for i in range(NT + 1):
            emit_loads(i)
            if i in BIAS_LOADS:
                bias_load(BIAS_LOADS[i])
            pre_vector(i + PA)
            if i >= 1:
                op, half, r, pair = tiles[i - 1]
                if op == "x":
                    quantize_x(i - 1)
                elif pair == 1:
                    quantize_w(half, r, 2)
            if i < NT:
                for a in range(4):
                    bank(i, a)
                    if a == 2:
                        for part in range(shares(i + PA)[1]):
                            pre_scalar(i + PA, part)
            for half, g_pass, t in mm_plan.get(i, []):
                if (half, t) not in accs:
                    alloc_acc(half, t)
                mm(half, g_pass, t)
            for item in bias_plan.get(i, []):
                if item[3] != 0:
                    bias_add(*item)
            if i < NT:
                op, half, r, pair = tiles[i]
                if op == "w" and pair == 1:
                    quantize_w(half, r, 0)
            for t in ev_plan.get(i, ()):
                ev_add(0, t)
            for item in bias_plan.get(i, []):
                if item[3] == 0:
                    bias_add(*item)
            for t in red_plan.get(i, ()):
                store0(0, t)
                ev_red(0, t)

        for upto in (14, 16):
            for t in (0, 1):
                for g_pass in range(done[t], upto):
                    mm(1, g_pass, t)
                done[t] = upto
        for t in (2, 3):
            for g_pass in range(done[t], 16):
                mm(1, g_pass, t)
        for t in (0, 1):
            ev_add(1, t)
            store0(1, t)
        for t in (0, 1):
            ev_red(1, t)
        for t in (0, 1):
            row_scale(t)
        factor(0)
        cast_store(0, 0)
        ev_add(1, 2)
        store0(1, 2)
        factor(1)
        cast_store(1, 0)
        ev_red(1, 2)
        row_scale(2)
        ev_add(1, 3)
        store0(1, 3)
        factor(2)
        cast_store(2, 0)
        ev_red(1, 3)
        row_scale(3)
        factor(3)
        cast_store(3, 640)
